import numpy as np
import ml_dtypes


def mxq(x, axis, fmt="e4m3"):
    dtype, down = {"e4m3": (ml_dtypes.float8_e4m3fn, 7), "e5m2": (ml_dtypes.float8_e5m2, 14)}[fmt]
    v = np.moveaxis(np.asarray(x, np.float32).astype(ml_dtypes.bfloat16).astype(np.float64), axis, -1)
    blocks = v.reshape(v.shape[:-1] + (-1, 32))
    amax = np.abs(blocks).max(-1, keepdims=True)
    byte = np.maximum(np.where(amax > 0, np.frexp(amax)[1] - 1 + 127, 0) - down, 1)
    scale = np.exp2(byte - 127.0)
    codes = (blocks / scale).astype(np.float32).astype(dtype).astype(np.float64)
    return np.moveaxis((codes * scale).reshape(v.shape), -1, axis)


WIDE = False


def mx_kscale(k):
    if not WIDE:
        return np.ones(k)
    levels = np.array([10, -10, 5, -5, 0])
    a = np.random.permutation(np.resize(levels, k // 512 * 4)).reshape(k // 512, 4)
    idx = np.arange(k)
    return np.exp2(a[idx // 512, idx % 128 // 32])


BF16 = ml_dtypes.bfloat16


def bf(x):
    return np.asarray(x, np.float32).astype(BF16)


def f64(x):
    return np.asarray(x).astype(np.float64)


B, C, D, H, W, W0, W1 = 16, 512, 128, 16, 32, 64, 256
N = H * W


def setup_inputs():
    s = mx_kscale(C)
    return {
        "x": bf(np.random.standard_normal((B, C, N))),
        "out1": bf(np.random.standard_normal((B, C, N)) * 0.6 * s[None, :, None]),
        "q": bf(np.random.standard_normal((B, N, D)) * 0.42),
        "k": bf(np.random.standard_normal((B, D, N)) * 0.42),
        "wv2": bf(np.random.standard_normal((C, C)) * 4.0 / np.sqrt(C) / s[None, :]),
        "bv2": bf(np.random.standard_normal(C) * 0.3),
        "gamma": bf(1.0 + 0.1 * np.random.standard_normal(1)),
    }


def reference(x, out1, q, k, wv2, bv2, gamma):
    val = (mxq(f64(wv2), 1, "e4m3") @ mxq(f64(out1), 1, "e4m3")) + f64(bv2)[None, :, None]
    s = f64(q) @ f64(k)
    e = np.exp(s - s.max(-1, keepdims=True))
    out = (mxq(val, 2, "e4m3") @ mxq(e, 2, "e4m3").transpose(0, 2, 1)) / e.sum(-1)[:, None, :]
    return f64(gamma)[0] * out + f64(x)

@@ -1,0 +1,268 @@
+from contextlib import ExitStack
+
+import concourse.mybir as mybir
+from concourse.masks import make_identity
+
+F32 = mybir.dt.float32
+BF16 = mybir.dt.bfloat16
+U32 = mybir.dt.uint32
+U8 = mybir.dt.uint8
+FP8X4 = mybir.dt.float8_e4m3fn_x4
+ALU = mybir.AluOpType
+ACT = mybir.ActivationFunctionType
+AXIS = mybir.AxisListType
+
+BATCH = 16
+C = 512
+N = 512
+D = 128
+P = 128
+PACK = 4
+TILES = N // P
+STEPS = BATCH * TILES
+
+FLOPS = 2 * BATCH * (C * C * N + N * N * D + C * N * N)
+
+
+def block(i):
+    return slice(i * P, (i + 1) * P)
+
+
+def tile_mvpam_module_mask_cascade_pb_t_kernel(tc, x, out1, q, k, wv2, bv2, gamma, out):
+    nc = tc.nc
+    with ExitStack() as ctx:
+        const = ctx.enter_context(tc.tile_pool(name="const", bufs=1))
+        two = ctx.enter_context(tc.tile_pool(name="two", bufs=2))
+        three = ctx.enter_context(tc.tile_pool(name="three", bufs=3))
+        ps_scores = ctx.enter_context(tc.psum_pool(name="ps_scores", bufs=2))
+        ps_turned = ctx.enter_context(tc.psum_pool(name="ps_turned", bufs=2))
+        ps_values = ctx.enter_context(tc.psum_pool(name="ps_values", bufs=1))
+        ps_att = ctx.enter_context(tc.psum_pool(name="ps_att", bufs=2))
+        ps_result = ctx.enter_context(tc.psum_pool(name="ps_result", bufs=1))
+        ctx.enter_context(tc.manual_schedule())
+
+        live = {}
+
+        w_rows = const.tile([P, TILES, C], BF16)
+        nc.sync.dma_start(out=w_rows[:], in_=wv2.rearrange("(ct p) ci -> p ct ci", p=P))
+        bias_rows = const.tile([P, C], BF16)
+        nc.scalar.dma_start(out=bias_rows[:], in_=bv2.partition_broadcast(P))
+        gamma_bf = const.tile([P, 1], BF16)
+        nc.scalar.dma_start(out=gamma_bf[:], in_=gamma.partition_broadcast(P))
+        ident_bf = const.tile([P, P], BF16)
+        make_identity(nc, ident_bf[:])
+        ident_f32 = const.tile([P, P], F32)
+        make_identity(nc, ident_f32[:])
+
+        def load_features(b):
+            feat_rows = three.tile([P, PACK, N], BF16)
+            nc.sync.dma_start(out=feat_rows[:], in_=out1[b].rearrange("(p j) n -> p j n", j=PACK))
+            live["feat_rows", b] = feat_rows
+            feat_grouped = two.tile([P, N, PACK], BF16, align_bytes=64)
+            live["feat_grouped", b] = feat_grouped
+
+        def load_queries_keys(b):
+            q_rows = two.tile([P, TILES, D], BF16)
+            nc.sync.dma_start(out=q_rows[:], in_=q[b].rearrange("(mt p) d -> p mt d", p=P))
+            live["q_rows", b] = q_rows
+            k_rows = three.tile([P, N], BF16)
+            nc.sync.dma_start(out=k_rows[:], in_=k[b])
+            live["k_rows", b] = k_rows
+
+        def load_residual(b):
+            x_rows = three.tile([P, TILES, N], BF16)
+            nc.sync.dma_start(out=x_rows[:], in_=x[b].rearrange("(ct p) m -> p ct m", p=P))
+            live["x_rows", b] = x_rows
+            result = three.tile([P, TILES, N], F32)
+            live["result", b] = result
+
+        def regroup_features(b, nt):
+            nc.vector.tensor_copy(
+                out=live["feat_grouped", b][:, block(nt), :].rearrange("p (n i) j -> p n j i", i=4),
+                in_=live["feat_rows", b][:, :, block(nt)].rearrange("p j (n i) -> p n j i", i=4),
+            )
+
+        def quantise_features(b):
+            feat_codes = two.tile([P, N], U32, align_bytes=64)
+            feat_scales = two.tile([P, N], U8, align_bytes=64)
+            nc.vector.quantize_mx(
+                out=feat_codes[:].bitcast(FP8X4),
+                scales=feat_scales[:],
+                in_=live["feat_grouped", b][:].rearrange("p n j -> p (n j)"),
+            )
+            live["feat_codes", b] = feat_codes
+            live["feat_scales", b] = feat_scales
+            val_grouped = two.tile([P, C, PACK], BF16, align_bytes=64)
+            live["val_grouped", b] = val_grouped
+
+        def values(b, ct):
+            val_ps = ps_values.tile([P, PACK, P], F32)
+            for t in range(PACK):
+                nc.tensor.matmul_mx(
+                    out=val_ps[:, t, :],
+                    lhsT=live["feat_codes", b][:, block(t)].bitcast(FP8X4),
+                    lhsT_scale=live["feat_scales", b][:, block(t)],
+                    rhs=w_codes[:, block(ct)].bitcast(FP8X4),
+                    rhs_scale=w_scales[:, block(ct)],
+                    start=True,
+                    stop=True,
+                )
+            nc.vector.tensor_tensor(
+                out=live["val_grouped", b][:, block(ct), :],
+                in0=val_ps[:].rearrange("p t c -> p c t"),
+                in1=bias_rows[:, block(ct)].unsqueeze(2).to_broadcast([P, P, PACK]),
+                op=ALU.add,
+            )
+
+        def quantise_values(b):
+            val_codes = two.tile([P, C], U32, align_bytes=64)
+            val_scales = two.tile([P, C], U8, align_bytes=64)
+            nc.vector.quantize_mx(
+                out=val_codes[:].bitcast(FP8X4),
+                scales=val_scales[:],
+                in_=live["val_grouped", b][:].rearrange("p c t -> p (c t)"),
+            )
+            live["val_codes", b] = val_codes
+            live["val_scales", b] = val_scales
+
+        def transpose_queries(b):
+            qt_ps = ps_turned.tile([P, TILES, P], BF16, tag="turned")
+            for mt in range(TILES):
+                nc.tensor.transpose(qt_ps[:, mt, :], live["q_rows", b][:, mt, :], ident_bf[:])
+            q_turned = two.tile([P, N], BF16)
+            nc.scalar.copy(out=q_turned[:], in_=qt_ps[:].rearrange("d mt m -> d (mt m)"))
+            live["q_turned", b] = q_turned
+
+        def scores(b, mt):
+            s_ps = ps_scores.tile([P, N], F32)
+            nc.tensor.matmul(
+                out=s_ps[:],
+                lhsT=live["q_turned", b][:, block(mt)],
+                rhs=live["k_rows", b][:],
+                start=True,
+                stop=True,
+            )
+            live["s_ps", b, mt] = s_ps
+
+        def softmax_numerator(b, mt):
+            s_ps = live["s_ps", b, mt]
+            neg_max = three.tile([P, 1], F32)
+            nc.vector.tensor_reduce(out=neg_max[:], in_=s_ps[:], axis=AXIS.X, op=ALU.max, negate=True)
+            e_rows = two.tile([P, N], BF16)
+            row_sum = three.tile([P, 1], F32)
+            nc.scalar.activation(
+                out=e_rows[:],
+                in_=s_ps[:],
+                func=ACT.Exp,
+                bias=neg_max[:],
+                scale=1.0,
+                accum_out=row_sum[:],
+            )
+            live["e_rows", b, mt] = e_rows
+            live["row_sum", b, mt] = row_sum
+
+        def keys_to_partitions(b, mt):
+            et_ps = ps_turned.tile([P, PACK, P], BF16, tag="turned")
+            for t in range(PACK):
+                nc.tensor.transpose(et_ps[:, t, :], live["e_rows", b, mt][:, block(t)], ident_bf[:])
+            e_grouped = two.tile([P, P, PACK], BF16, align_bytes=64)
+            nc.scalar.copy(out=e_grouped[:], in_=et_ps[:].rearrange("p t m -> p m t"))
+            live["e_grouped", b, mt] = e_grouped
+
+        def quantise_e(b, mt):
+            inv_sum = three.tile([P, 1], F32)
+            nc.vector.reciprocal(out=inv_sum[:], in_=live["row_sum", b, mt][:])
+            live["inv_sum", b, mt] = inv_sum
+            e_codes = two.tile([P, P], U32, align_bytes=64)
+            e_scales = two.tile([P, P], U8, align_bytes=64)
+            nc.vector.quantize_mx(
+                out=e_codes[:].bitcast(FP8X4),
+                scales=e_scales[:],
+                in_=live["e_grouped", b, mt][:].rearrange("p m t -> p (m t)"),
+            )
+            live["e_codes", b, mt] = e_codes
+            live["e_scales", b, mt] = e_scales
+
+        def attend(b, mt):
+            att_ps = ps_att.tile([P, C], F32)
+            nc.tensor.matmul_mx(
+                out=att_ps[:],
+                lhsT=live["e_codes", b, mt][:].bitcast(FP8X4),
+                lhsT_scale=live["e_scales", b, mt][:],
+                rhs=live["val_codes", b][:].bitcast(FP8X4),
+                rhs_scale=live["val_scales", b][:],
+                start=True,
+                stop=True,
+            )
+            live["att_ps", b, mt] = att_ps
+
+        def normalise(b, mt):
+            att_rows = two.tile([P, C], F32)
+            nc.scalar.activation(
+                out=att_rows[:],
+                in_=live["att_ps", b, mt][:],
+                func=ACT.Copy,
+                scale=live["inv_sum", b, mt][:],
+            )
+            live["att_rows", b, mt] = att_rows
+
+        def finish(b, mt):
+            result_ps = ps_result.tile([P, TILES, P], F32)
+            for ct in range(TILES):
+                nc.tensor.transpose(
+                    result_ps[:, ct, :], live["att_rows", b, mt][:, block(ct)], ident_f32[:]
+                )
+            nc.vector.scalar_tensor_tensor(
+                out=live["result", b][:, :, block(mt)],
+                in0=result_ps[:],
+                scalar=gamma_col[:],
+                in1=live["x_rows", b][:, :, block(mt)],
+                op0=ALU.mult,
+                op1=ALU.add,
+            )
+            if mt == TILES - 1:
+                nc.sync.dma_start(
+                    out=out[b].rearrange("(ct p) m -> p ct m", p=P), in_=live["result", b][:]
+                )
+
+        w_grouped = const.tile([P, C, PACK], BF16, align_bytes=64)
+        for ct in range(TILES):
+            wt_ps = ps_turned.tile([P, PACK, P], BF16, tag="turned")
+            every_fourth = w_rows[:, ct, :].rearrange("c (p j) -> c j p", j=PACK)
+            for j in range(PACK):
+                nc.tensor.transpose(wt_ps[:, j, :], every_fourth[:, j, :], ident_bf[:])
+            nc.scalar.copy(out=w_grouped[:, block(ct), :], in_=wt_ps[:].rearrange("p j c -> p c j"))
+        w_codes = const.tile([P, C], U32, align_bytes=64)
+        w_scales = const.tile([P, C], U8, align_bytes=64)
+        nc.vector.quantize_mx(
+            out=w_codes[:].bitcast(FP8X4),
+            scales=w_scales[:],
+            in_=w_grouped[:].rearrange("p c j -> p (c j)"),
+        )
+        gamma_col = const.tile([P, 1], F32)
+        nc.vector.tensor_copy(out=gamma_col[:], in_=gamma_bf[:])
+
+        def for_tile(stage, step):
+            if 0 <= step < STEPS:
+                stage(*divmod(step, TILES))
+
+        def for_batch(stage, step):
+            if 0 <= step < STEPS and step % TILES == 0:
+                stage(step // TILES)
+
+        for i in range(-3 * TILES, STEPS + 3):
+            for_batch(load_features, i + 12)
+            for_batch(load_queries_keys, i + 7)
+            for_batch(load_residual, i + 2)
+            for_tile(scores, i + 1)
+            for_tile(softmax_numerator, i)
+            for_tile(quantise_e, i - 1)
+            for_batch(quantise_values, i)
+            for_tile(finish, i - 3)
+            for_batch(transpose_queries, i + 2)
+            for_tile(regroup_features, i + 9)
+            for_tile(values, i + 4)
+            for_tile(attend, i - 1)
+            for_tile(normalise, i - 2)
+            for_tile(keys_to_partitions, i)
+            for_batch(quantise_features, i + 5)

@@ -34,6 +34,7 @@ def tile_mvpam_module_mask_cascade_pb_t_kernel(tc, x, out1, q, k, wv2, bv2, gamm
         const = ctx.enter_context(tc.tile_pool(name="const", bufs=1))
         two = ctx.enter_context(tc.tile_pool(name="two", bufs=2))
         three = ctx.enter_context(tc.tile_pool(name="three", bufs=3))
+        four = ctx.enter_context(tc.tile_pool(name="four", bufs=4))
         ps_scores = ctx.enter_context(tc.psum_pool(name="ps_scores", bufs=2))
         ps_turned = ctx.enter_context(tc.psum_pool(name="ps_turned", bufs=2))
         ps_values = ctx.enter_context(tc.psum_pool(name="ps_values", bufs=1))
@@ -58,8 +59,6 @@ def tile_mvpam_module_mask_cascade_pb_t_kernel(tc, x, out1, q, k, wv2, bv2, gamm
             feat_rows = three.tile([P, PACK, N], BF16)
             nc.sync.dma_start(out=feat_rows[:], in_=out1[b].rearrange("(p j) n -> p j n", j=PACK))
             live["feat_rows", b] = feat_rows
-            feat_grouped = two.tile([P, N, PACK], BF16, align_bytes=64)
-            live["feat_grouped", b] = feat_grouped
 
         def load_queries_keys(b):
             q_rows = two.tile([P, TILES, D], BF16)
@@ -77,9 +76,16 @@ def tile_mvpam_module_mask_cascade_pb_t_kernel(tc, x, out1, q, k, wv2, bv2, gamm
             live["result", b] = result
 
         def regroup_features(b, nt):
-            nc.vector.tensor_copy(
-                out=live["feat_grouped", b][:, block(nt), :].rearrange("p (n i) j -> p n j i", i=4),
-                in_=live["feat_rows", b][:, :, block(nt)].rearrange("p j (n i) -> p n j i", i=4),
+            if nt == 0:
+                feat_grouped = two.tile([P, N, PACK], BF16, align_bytes=64)
+                live["feat_grouped", b] = feat_grouped
+            nc.gpsimd.tensor_scalar(
+                out=live["feat_grouped", b][:, block(nt), :],
+                in0=live["feat_rows", b][:, :, block(nt)].rearrange("p j n -> p n j"),
+                scalar1=1.0,
+                scalar2=0.0,
+                op0=ALU.mult,
+                op1=ALU.add,
             )
 
         def quantise_features(b):
@@ -144,22 +150,31 @@ def tile_mvpam_module_mask_cascade_pb_t_kernel(tc, x, out1, q, k, wv2, bv2, gamm
             )
             live["s_ps", b, mt] = s_ps
 
-        def softmax_numerator(b, mt):
-            s_ps = live["s_ps", b, mt]
+        def row_maximum(b, mt):
             neg_max = three.tile([P, 1], F32)
-            nc.vector.tensor_reduce(out=neg_max[:], in_=s_ps[:], axis=AXIS.X, op=ALU.max, negate=True)
+            nc.vector.tensor_reduce(
+                out=neg_max[:], in_=live["s_ps", b, mt][:], axis=AXIS.X, op=ALU.max, negate=True
+            )
+            live["neg_max", b, mt] = neg_max
+
+        def exponentials(b, mt):
             e_rows = two.tile([P, N], BF16)
             row_sum = three.tile([P, 1], F32)
             nc.scalar.activation(
                 out=e_rows[:],
-                in_=s_ps[:],
+                in_=live["s_ps", b, mt][:],
                 func=ACT.Exp,
-                bias=neg_max[:],
+                bias=live["neg_max", b, mt][:],
                 scale=1.0,
                 accum_out=row_sum[:],
             )
             live["e_rows", b, mt] = e_rows
             live["row_sum", b, mt] = row_sum
+
+        def invert_row_sum(b, mt):
+            inv_sum = four.tile([P, 1], F32)
+            nc.vector.reciprocal(out=inv_sum[:], in_=live["row_sum", b, mt][:])
+            live["inv_sum", b, mt] = inv_sum
 
         def keys_to_partitions(b, mt):
             et_ps = ps_turned.tile([P, PACK, P], BF16, tag="turned")
@@ -170,9 +185,6 @@ def tile_mvpam_module_mask_cascade_pb_t_kernel(tc, x, out1, q, k, wv2, bv2, gamm
             live["e_grouped", b, mt] = e_grouped
 
         def quantise_e(b, mt):
-            inv_sum = three.tile([P, 1], F32)
-            nc.vector.reciprocal(out=inv_sum[:], in_=live["row_sum", b, mt][:])
-            live["inv_sum", b, mt] = inv_sum
             e_codes = two.tile([P, P], U32, align_bytes=64)
             e_scales = two.tile([P, P], U8, align_bytes=64)
             nc.vector.quantize_mx(
@@ -220,10 +232,10 @@ def tile_mvpam_module_mask_cascade_pb_t_kernel(tc, x, out1, q, k, wv2, bv2, gamm
                 op0=ALU.mult,
                 op1=ALU.add,
             )
-            if mt == TILES - 1:
-                nc.sync.dma_start(
-                    out=out[b].rearrange("(ct p) m -> p ct m", p=P), in_=live["result", b][:]
-                )
+            nc.sync.dma_start(
+                out=out[b].rearrange("(ct p) m -> p ct m", p=P)[:, :, block(mt)],
+                in_=live["result", b][:, :, block(mt)],
+            )
 
         w_grouped = const.tile([P, C, PACK], BF16, align_bytes=64)
         for ct in range(TILES):
@@ -250,19 +262,21 @@ def tile_mvpam_module_mask_cascade_pb_t_kernel(tc, x, out1, q, k, wv2, bv2, gamm
             if 0 <= step < STEPS and step % TILES == 0:
                 stage(step // TILES)
 
-        for i in range(-3 * TILES, STEPS + 3):
-            for_batch(load_features, i + 12)
-            for_batch(load_queries_keys, i + 7)
-            for_batch(load_residual, i + 2)
+        for i in range(-14, STEPS + 5):
+            for_batch(load_features, i + 14)
+            for_batch(load_queries_keys, i + 8)
+            for_batch(load_residual, i)
             for_tile(scores, i + 1)
-            for_tile(softmax_numerator, i)
-            for_tile(quantise_e, i - 1)
-            for_batch(quantise_values, i)
-            for_tile(finish, i - 3)
-            for_batch(transpose_queries, i + 2)
-            for_tile(regroup_features, i + 9)
-            for_tile(values, i + 4)
-            for_tile(attend, i - 1)
-            for_tile(normalise, i - 2)
-            for_tile(keys_to_partitions, i)
-            for_batch(quantise_features, i + 5)
+            for_tile(row_maximum, i + 1)
+            for_tile(exponentials, i)
+            for_tile(keys_to_partitions, i - 1)
+            for_tile(invert_row_sum, i - 1)
+            for_tile(quantise_e, i - 2)
+            for_tile(finish, i - 5)
+            for_batch(transpose_queries, i + 4)
+            for_tile(normalise, i - 4)
+            for_tile(regroup_features, i + 10)
+            for_tile(values, i + 3)
+            for_tile(attend, i - 3)
+            for_batch(quantise_values, i - 2)
+            for_batch(quantise_features, i + 4)

@@ -37,9 +37,8 @@ def tile_mvpam_module_mask_cascade_pb_t_kernel(tc, x, out1, q, k, wv2, bv2, gamm
         four = ctx.enter_context(tc.tile_pool(name="four", bufs=4))
         ps_scores = ctx.enter_context(tc.psum_pool(name="ps_scores", bufs=2))
         ps_turned = ctx.enter_context(tc.psum_pool(name="ps_turned", bufs=2))
-        ps_values = ctx.enter_context(tc.psum_pool(name="ps_values", bufs=1))
         ps_att = ctx.enter_context(tc.psum_pool(name="ps_att", bufs=2))
-        ps_result = ctx.enter_context(tc.psum_pool(name="ps_result", bufs=1))
+        ps_quarters = ctx.enter_context(tc.psum_pool(name="ps_quarters", bufs=2))
         ctx.enter_context(tc.manual_schedule())
 
         live = {}
@@ -79,7 +78,8 @@ def tile_mvpam_module_mask_cascade_pb_t_kernel(tc, x, out1, q, k, wv2, bv2, gamm
             if nt == 0:
                 feat_grouped = two.tile([P, N, PACK], BF16, align_bytes=64)
                 live["feat_grouped", b] = feat_grouped
-            nc.gpsimd.tensor_scalar(
+            mover = nc.vector if b == 0 else nc.gpsimd
+            mover.tensor_scalar(
                 out=live["feat_grouped", b][:, block(nt), :],
                 in0=live["feat_rows", b][:, :, block(nt)].rearrange("p j n -> p n j"),
                 scalar1=1.0,
@@ -102,7 +102,7 @@ def tile_mvpam_module_mask_cascade_pb_t_kernel(tc, x, out1, q, k, wv2, bv2, gamm
             live["val_grouped", b] = val_grouped
 
         def values(b, ct):
-            val_ps = ps_values.tile([P, PACK, P], F32)
+            val_ps = ps_quarters.tile([P, PACK, P], F32, tag="quarters")
             for t in range(PACK):
                 nc.tensor.matmul_mx(
                     out=val_ps[:, t, :],
@@ -158,49 +158,53 @@ def tile_mvpam_module_mask_cascade_pb_t_kernel(tc, x, out1, q, k, wv2, bv2, gamm
             live["neg_max", b, mt] = neg_max
 
         def exponentials(b, mt):
-            e_rows = two.tile([P, N], BF16)
-            row_sum = three.tile([P, 1], F32)
+            if mt == 0:
+                row_sums = three.tile([P, TILES], F32)
+                live["row_sums", b] = row_sums
+            e_rows = four.tile([P, N], BF16)
             nc.scalar.activation(
                 out=e_rows[:],
                 in_=live["s_ps", b, mt][:],
                 func=ACT.Exp,
                 bias=live["neg_max", b, mt][:],
                 scale=1.0,
-                accum_out=row_sum[:],
+                accum_out=live["row_sums", b][:, mt : mt + 1],
             )
             live["e_rows", b, mt] = e_rows
-            live["row_sum", b, mt] = row_sum
 
-        def invert_row_sum(b, mt):
-            inv_sum = four.tile([P, 1], F32)
-            nc.vector.reciprocal(out=inv_sum[:], in_=live["row_sum", b, mt][:])
-            live["inv_sum", b, mt] = inv_sum
+        def invert_row_sums(b):
+            inv_sums = three.tile([P, TILES], F32)
+            nc.vector.reciprocal(out=inv_sums[:], in_=live["row_sums", b][:])
+            live["inv_sums", b] = inv_sums
 
-        def keys_to_partitions(b, mt):
-            et_ps = ps_turned.tile([P, PACK, P], BF16, tag="turned")
-            for t in range(PACK):
-                nc.tensor.transpose(et_ps[:, t, :], live["e_rows", b, mt][:, block(t)], ident_bf[:])
-            e_grouped = two.tile([P, P, PACK], BF16, align_bytes=64)
-            nc.scalar.copy(out=e_grouped[:], in_=et_ps[:].rearrange("p t m -> p m t"))
-            live["e_grouped", b, mt] = e_grouped
+        def keys_to_partitions(b, pair):
+            et_ps = ps_turned.tile([P, 2, PACK, P], BF16, tag="turned")
+            for u in range(2):
+                for t in range(PACK):
+                    nc.tensor.transpose(
+                        et_ps[:, u, t, :], live["e_rows", b, 2 * pair + u][:, block(t)], ident_bf[:]
+                    )
+            e_grouped = two.tile([P, 2, P, PACK], BF16, align_bytes=64)
+            nc.scalar.copy(out=e_grouped[:], in_=et_ps[:].rearrange("p u t m -> p u m t"))
+            live["e_grouped", b, pair] = e_grouped
 
-        def quantise_e(b, mt):
-            e_codes = two.tile([P, P], U32, align_bytes=64)
-            e_scales = two.tile([P, P], U8, align_bytes=64)
+        def quantise_e(b, pair):
+            e_codes = two.tile([P, 2 * P], U32, align_bytes=64)
+            e_scales = two.tile([P, 2 * P], U8, align_bytes=64)
             nc.vector.quantize_mx(
                 out=e_codes[:].bitcast(FP8X4),
                 scales=e_scales[:],
-                in_=live["e_grouped", b, mt][:].rearrange("p m t -> p (m t)"),
+                in_=live["e_grouped", b, pair][:].rearrange("p u m t -> p (u m t)"),
             )
-            live["e_codes", b, mt] = e_codes
-            live["e_scales", b, mt] = e_scales
+            live["e_codes", b, pair] = e_codes
+            live["e_scales", b, pair] = e_scales
 
         def attend(b, mt):
             att_ps = ps_att.tile([P, C], F32)
             nc.tensor.matmul_mx(
                 out=att_ps[:],
-                lhsT=live["e_codes", b, mt][:].bitcast(FP8X4),
-                lhsT_scale=live["e_scales", b, mt][:],
+                lhsT=live["e_codes", b, mt // 2][:, block(mt % 2)].bitcast(FP8X4),
+                lhsT_scale=live["e_scales", b, mt // 2][:, block(mt % 2)],
                 rhs=live["val_codes", b][:].bitcast(FP8X4),
                 rhs_scale=live["val_scales", b][:],
                 start=True,
@@ -214,12 +218,12 @@ def tile_mvpam_module_mask_cascade_pb_t_kernel(tc, x, out1, q, k, wv2, bv2, gamm
                 out=att_rows[:],
                 in_=live["att_ps", b, mt][:],
                 func=ACT.Copy,
-                scale=live["inv_sum", b, mt][:],
+                scale=live["inv_sums", b][:, mt : mt + 1],
             )
             live["att_rows", b, mt] = att_rows
 
         def finish(b, mt):
-            result_ps = ps_result.tile([P, TILES, P], F32)
+            result_ps = ps_quarters.tile([P, TILES, P], F32, tag="quarters")
             for ct in range(TILES):
                 nc.tensor.transpose(
                     result_ps[:, ct, :], live["att_rows", b, mt][:, block(ct)], ident_f32[:]
@@ -238,45 +242,55 @@ def tile_mvpam_module_mask_cascade_pb_t_kernel(tc, x, out1, q, k, wv2, bv2, gamm
             )
 
         w_grouped = const.tile([P, C, PACK], BF16, align_bytes=64)
-        for ct in range(TILES):
-            wt_ps = ps_turned.tile([P, PACK, P], BF16, tag="turned")
-            every_fourth = w_rows[:, ct, :].rearrange("c (p j) -> c j p", j=PACK)
-            for j in range(PACK):
-                nc.tensor.transpose(wt_ps[:, j, :], every_fourth[:, j, :], ident_bf[:])
-            nc.scalar.copy(out=w_grouped[:, block(ct), :], in_=wt_ps[:].rearrange("p j c -> p c j"))
         w_codes = const.tile([P, C], U32, align_bytes=64)
         w_scales = const.tile([P, C], U8, align_bytes=64)
-        nc.vector.quantize_mx(
-            out=w_codes[:].bitcast(FP8X4),
-            scales=w_scales[:],
-            in_=w_grouped[:].rearrange("p c j -> p (c j)"),
-        )
         gamma_col = const.tile([P, 1], F32)
-        nc.vector.tensor_copy(out=gamma_col[:], in_=gamma_bf[:])
+
+        def prepare_weights():
+            for ct in range(TILES):
+                wt_ps = ps_turned.tile([P, PACK, P], BF16, tag="turned")
+                every_fourth = w_rows[:, ct, :].rearrange("c (p j) -> c j p", j=PACK)
+                for j in range(PACK):
+                    nc.tensor.transpose(wt_ps[:, j, :], every_fourth[:, j, :], ident_bf[:])
+                nc.scalar.copy(
+                    out=w_grouped[:, block(ct), :], in_=wt_ps[:].rearrange("p j c -> p c j")
+                )
+            nc.vector.quantize_mx(
+                out=w_codes[:].bitcast(FP8X4),
+                scales=w_scales[:],
+                in_=w_grouped[:].rearrange("p c j -> p (c j)"),
+            )
+            nc.vector.tensor_copy(out=gamma_col[:], in_=gamma_bf[:])
 
         def for_tile(stage, step):
             if 0 <= step < STEPS:
                 stage(*divmod(step, TILES))
 
+        def for_pair(stage, step):
+            if 0 <= step < STEPS and step % 2 == 0:
+                stage(step // TILES, (step % TILES) // 2)
+
         def for_batch(stage, step):
             if 0 <= step < STEPS and step % TILES == 0:
                 stage(step // TILES)
 
-        for i in range(-14, STEPS + 5):
+        for i in range(-14, STEPS + 7):
             for_batch(load_features, i + 14)
             for_batch(load_queries_keys, i + 8)
             for_batch(load_residual, i)
+            if i == -5:
+                prepare_weights()
             for_tile(scores, i + 1)
             for_tile(row_maximum, i + 1)
             for_tile(exponentials, i)
-            for_tile(keys_to_partitions, i - 1)
-            for_tile(invert_row_sum, i - 1)
-            for_tile(quantise_e, i - 2)
-            for_tile(finish, i - 5)
+            for_pair(keys_to_partitions, i - 2)
+            for_batch(invert_row_sums, i - 4)
+            for_pair(quantise_e, i - 3)
+            for_tile(finish, i - 6)
             for_batch(transpose_queries, i + 4)
-            for_tile(normalise, i - 4)
+            for_tile(normalise, i - 5)
             for_tile(regroup_features, i + 10)
             for_tile(values, i + 3)
-            for_tile(attend, i - 3)
+            for_tile(attend, i - 4)
             for_batch(quantise_values, i - 2)
             for_batch(quantise_features, i + 4)

@@ -28,6 +28,11 @@ def block(i):
     return slice(i * P, (i + 1) * P)
 
 
+def key_pairs(t):
+    u, e = divmod(t, 2)
+    return slice(2 * P * u + e, 2 * P * (u + 1), 2)
+
+
 def tile_mvpam_module_mask_cascade_pb_t_kernel(tc, x, out1, q, k, wv2, bv2, gamma, out):
     nc = tc.nc
     with ExitStack() as ctx:
@@ -78,15 +83,12 @@ def tile_mvpam_module_mask_cascade_pb_t_kernel(tc, x, out1, q, k, wv2, bv2, gamm
             if nt == 0:
                 feat_grouped = two.tile([P, N, PACK], BF16, align_bytes=64)
                 live["feat_grouped", b] = feat_grouped
-            mover = nc.vector if b == 0 else nc.gpsimd
-            mover.tensor_scalar(
-                out=live["feat_grouped", b][:, block(nt), :],
-                in0=live["feat_rows", b][:, :, block(nt)].rearrange("p j n -> p n j"),
-                scalar1=1.0,
-                scalar2=0.0,
-                op0=ALU.mult,
-                op1=ALU.add,
-            )
+            grouped = live["feat_grouped", b][:, block(nt), :]
+            rows = live["feat_rows", b][:, :, key_pairs(nt)].rearrange("p j n -> p n j")
+            if b == 0:
+                nc.vector.tensor_copy(out=grouped, in_=rows)
+            else:
+                nc.scalar.copy(out=grouped, in_=rows)
 
         def quantise_features(b):
             feat_codes = two.tile([P, N], U32, align_bytes=64)
@@ -178,68 +180,76 @@ def tile_mvpam_module_mask_cascade_pb_t_kernel(tc, x, out1, q, k, wv2, bv2, gamm
             live["inv_sums", b] = inv_sums
 
         def keys_to_partitions(b, pair):
-            et_ps = ps_turned.tile([P, 2, PACK, P], BF16, tag="turned")
-            for u in range(2):
-                for t in range(PACK):
-                    nc.tensor.transpose(
-                        et_ps[:, u, t, :], live["e_rows", b, 2 * pair + u][:, block(t)], ident_bf[:]
-                    )
+            et_ps = ps_turned.tile([P, 2, 2, P], F32, tag="turned")
+            for a in range(2):
+                e_words = live["e_rows", b, 2 * pair + a][:].bitcast(F32)
+                for u in range(2):
+                    nc.tensor.transpose(et_ps[:, a, u, :], e_words[:, block(u)], ident_f32[:])
             e_grouped = two.tile([P, 2, P, PACK], BF16, align_bytes=64)
-            nc.scalar.copy(out=e_grouped[:], in_=et_ps[:].rearrange("p u t m -> p u m t"))
+            nc.scalar.copy(
+                out=e_grouped[:].bitcast(F32), in_=et_ps[:].rearrange("p a u m -> p a m u")
+            )
             live["e_grouped", b, pair] = e_grouped
 
         def quantise_e(b, pair):
-            e_codes = two.tile([P, 2 * P], U32, align_bytes=64)
-            e_scales = two.tile([P, 2 * P], U8, align_bytes=64)
+            if pair == 0:
+                e_codes = two.tile([P, N], U32, align_bytes=64)
+                e_scales = two.tile([P, N], U8, align_bytes=64)
+                live["e_codes", b] = e_codes
+                live["e_scales", b] = e_scales
+            queries = slice(pair * 2 * P, (pair + 1) * 2 * P)
             nc.vector.quantize_mx(
-                out=e_codes[:].bitcast(FP8X4),
-                scales=e_scales[:],
-                in_=live["e_grouped", b, pair][:].rearrange("p u m t -> p (u m t)"),
+                out=live["e_codes", b][:, queries].bitcast(FP8X4),
+                scales=live["e_scales", b][:, queries],
+                in_=live["e_grouped", b, pair][:].rearrange("p a m t -> p (a m t)"),
             )
-            live["e_codes", b, pair] = e_codes
-            live["e_scales", b, pair] = e_scales
 
-        def attend(b, mt):
-            att_ps = ps_att.tile([P, C], F32)
+        def spread_factors(b):
+            factors_ps = ps_turned.tile([P, TILES, P], F32, tag="turned")
+            for mt in range(TILES):
+                nc.tensor.transpose(
+                    factors_ps[:, mt, :],
+                    live["inv_sums", b][:, mt : mt + 1].to_broadcast([P, P]),
+                    ident_f32[:],
+                )
+            factors = two.tile([P, N], F32)
+            nc.scalar.activation(
+                out=factors[:],
+                in_=factors_ps[:].rearrange("p mt m -> p (mt m)"),
+                func=ACT.Copy,
+                scale=gamma_col[:],
+            )
+            live["factors", b] = factors
+
+        def attend(b, ct):
+            att_ps = ps_att.tile([P, N], F32)
             nc.tensor.matmul_mx(
                 out=att_ps[:],
-                lhsT=live["e_codes", b, mt // 2][:, block(mt % 2)].bitcast(FP8X4),
-                lhsT_scale=live["e_scales", b, mt // 2][:, block(mt % 2)],
-                rhs=live["val_codes", b][:].bitcast(FP8X4),
-                rhs_scale=live["val_scales", b][:],
+                lhsT=live["val_codes", b][:, block(ct)].bitcast(FP8X4),
+                lhsT_scale=live["val_scales", b][:, block(ct)],
+                rhs=live["e_codes", b][:].bitcast(FP8X4),
+                rhs_scale=live["e_scales", b][:],
                 start=True,
                 stop=True,
             )
-            live["att_ps", b, mt] = att_ps
+            live["att_ps", b, ct] = att_ps
 
-        def normalise(b, mt):
-            att_rows = two.tile([P, C], F32)
-            nc.scalar.activation(
-                out=att_rows[:],
-                in_=live["att_ps", b, mt][:],
-                func=ACT.Copy,
-                scale=live["inv_sums", b][:, mt : mt + 1],
+        def scale(b, ct):
+            nc.vector.tensor_tensor(
+                out=live["result", b][:, ct, :],
+                in0=live["att_ps", b, ct][:],
+                in1=live["factors", b][:],
+                op=ALU.mult,
             )
-            live["att_rows", b, mt] = att_rows
 
-        def finish(b, mt):
-            result_ps = ps_quarters.tile([P, TILES, P], F32, tag="quarters")
-            for ct in range(TILES):
-                nc.tensor.transpose(
-                    result_ps[:, ct, :], live["att_rows", b, mt][:, block(ct)], ident_f32[:]
-                )
-            nc.vector.scalar_tensor_tensor(
-                out=live["result", b][:, :, block(mt)],
-                in0=result_ps[:],
-                scalar=gamma_col[:],
-                in1=live["x_rows", b][:, :, block(mt)],
-                op0=ALU.mult,
-                op1=ALU.add,
+        def add_residual(b, ct):
+            nc.gpsimd.tensor_tensor(
+                out=live["result", b][:, ct, :],
+                in0=live["result", b][:, ct, :],
+                in1=live["x_rows", b][:, ct, :],
+                op=ALU.add,
             )
-            nc.sync.dma_start(
-                out=out[b].rearrange("(ct p) m -> p ct m", p=P)[:, :, block(mt)],
-                in_=live["result", b][:, :, block(mt)],
-            )
+            nc.sync.dma_start(out=out[b, block(ct), :], in_=live["result", b][:, ct, :])
 
         w_grouped = const.tile([P, C, PACK], BF16, align_bytes=64)
         w_codes = const.tile([P, C], U32, align_bytes=64)
@@ -274,23 +284,24 @@ def tile_mvpam_module_mask_cascade_pb_t_kernel(tc, x, out1, q, k, wv2, bv2, gamm
             if 0 <= step < STEPS and step % TILES == 0:
                 stage(step // TILES)
 
-        for i in range(-14, STEPS + 7):
+        for i in range(-14, STEPS + 8):
             for_batch(load_features, i + 14)
-            for_batch(load_queries_keys, i + 8)
+            for_batch(load_queries_keys, i + 10)
             for_batch(load_residual, i)
             if i == -5:
                 prepare_weights()
             for_tile(scores, i + 1)
-            for_tile(row_maximum, i + 1)
-            for_tile(exponentials, i)
-            for_pair(keys_to_partitions, i - 2)
-            for_batch(invert_row_sums, i - 4)
             for_pair(quantise_e, i - 3)
-            for_tile(finish, i - 6)
-            for_batch(transpose_queries, i + 4)
-            for_tile(normalise, i - 5)
-            for_tile(regroup_features, i + 10)
-            for_tile(values, i + 3)
-            for_tile(attend, i - 4)
             for_batch(quantise_values, i - 2)
             for_batch(quantise_features, i + 4)
+            for_batch(invert_row_sums, i - 4)
+            for_tile(scale, i - 7)
+            for_tile(add_residual, i - 7)
+            for_tile(row_maximum, i + 1)
+            for_tile(exponentials, i)
+            for_tile(values, i + 3)
+            for_tile(attend, i - 6)
+            for_tile(regroup_features, i + 8)
+            for_pair(keys_to_partitions, i - 2)
+            for_batch(transpose_queries, i + 5)
+            for_batch(spread_factors, i - 5)

@@ -28,11 +28,6 @@ def block(i):
     return slice(i * P, (i + 1) * P)
 
 
-def key_pairs(t):
-    u, e = divmod(t, 2)
-    return slice(2 * P * u + e, 2 * P * (u + 1), 2)
-
-
 def tile_mvpam_module_mask_cascade_pb_t_kernel(tc, x, out1, q, k, wv2, bv2, gamma, out):
     nc = tc.nc
     with ExitStack() as ctx:
@@ -84,7 +79,7 @@ def tile_mvpam_module_mask_cascade_pb_t_kernel(tc, x, out1, q, k, wv2, bv2, gamm
                 feat_grouped = two.tile([P, N, PACK], BF16, align_bytes=64)
                 live["feat_grouped", b] = feat_grouped
             grouped = live["feat_grouped", b][:, block(nt), :]
-            rows = live["feat_rows", b][:, :, key_pairs(nt)].rearrange("p j n -> p n j")
+            rows = live["feat_rows", b][:, :, block(nt)].rearrange("p j n -> p n j")
             if b == 0:
                 nc.vector.tensor_copy(out=grouped, in_=rows)
             else:
@@ -165,8 +160,8 @@ def tile_mvpam_module_mask_cascade_pb_t_kernel(tc, x, out1, q, k, wv2, bv2, gamm
                 live["row_sums", b] = row_sums
             e_rows = four.tile([P, N], BF16)
             nc.scalar.activation(
-                out=e_rows[:],
-                in_=live["s_ps", b, mt][:],
+                out=e_rows[:].rearrange("p (u w e) -> p u w e", u=2, e=2),
+                in_=live["s_ps", b, mt][:].rearrange("p (u e w) -> p u w e", u=2, e=2),
                 func=ACT.Exp,
                 bias=live["neg_max", b, mt][:],
                 scale=1.0,
@@ -291,12 +286,12 @@ def tile_mvpam_module_mask_cascade_pb_t_kernel(tc, x, out1, q, k, wv2, bv2, gamm
             if i == -5:
                 prepare_weights()
             for_tile(scores, i + 1)
+            for_tile(scale, i - 7)
+            for_tile(add_residual, i - 7)
             for_pair(quantise_e, i - 3)
             for_batch(quantise_values, i - 2)
             for_batch(quantise_features, i + 4)
             for_batch(invert_row_sums, i - 4)
-            for_tile(scale, i - 7)
-            for_tile(add_residual, i - 7)
             for_tile(row_maximum, i + 1)
             for_tile(exponentials, i)
             for_tile(values, i + 3)

@@ -20,6 +20,7 @@ P = 128
 PACK = 4
 TILES = N // P
 STEPS = BATCH * TILES
+BY_ROWS = 2
 
 FLOPS = 2 * BATCH * (C * C * N + N * N * D + C * N * N)
 
@@ -44,7 +45,6 @@ def tile_mvpam_module_mask_cascade_pb_t_kernel(tc, x, out1, q, k, wv2, bv2, gamm
         live = {}
 
         w_rows = const.tile([P, TILES, C], BF16)
-        nc.sync.dma_start(out=w_rows[:], in_=wv2.rearrange("(ct p) ci -> p ct ci", p=P))
         bias_rows = const.tile([P, C], BF16)
         nc.scalar.dma_start(out=bias_rows[:], in_=bv2.partition_broadcast(P))
         gamma_bf = const.tile([P, 1], BF16)
@@ -99,6 +99,8 @@ def tile_mvpam_module_mask_cascade_pb_t_kernel(tc, x, out1, q, k, wv2, bv2, gamm
             live["val_grouped", b] = val_grouped
 
         def values(b, ct):
+            if ct == BY_ROWS:
+                return
             val_ps = ps_quarters.tile([P, PACK, P], F32, tag="quarters")
             for t in range(PACK):
                 nc.tensor.matmul_mx(
@@ -115,6 +117,37 @@ def tile_mvpam_module_mask_cascade_pb_t_kernel(tc, x, out1, q, k, wv2, bv2, gamm
                 in0=val_ps[:].rearrange("p t c -> p c t"),
                 in1=bias_rows[:, block(ct)].unsqueeze(2).to_broadcast([P, P, PACK]),
                 op=ALU.add,
+            )
+
+        def value_rows(b):
+            val_ps = ps_quarters.tile([P, N], F32, tag="quarters")
+            nc.tensor.matmul_mx(
+                out=val_ps[:],
+                lhsT=w_codes[:, block(BY_ROWS)].bitcast(FP8X4),
+                lhsT_scale=w_scales[:, block(BY_ROWS)],
+                rhs=live["feat_codes", b][:].bitcast(FP8X4),
+                rhs_scale=live["feat_scales", b][:],
+                start=True,
+                stop=True,
+            )
+            val_rows = two.tile([P, N], BF16)
+            nc.scalar.activation(
+                out=val_rows[:].rearrange("p (u w e) -> p u w e", u=2, e=2),
+                in_=val_ps[:].rearrange("p (u e w) -> p u w e", u=2, e=2),
+                func=ACT.Identity,
+                bias=bias_col[:],
+                scale=1.0,
+            )
+            live["val_rows", b] = val_rows
+
+        def rows_to_keys(b):
+            vt_ps = ps_turned.tile([P, 2, P], F32, tag="turned")
+            val_words = live["val_rows", b][:].bitcast(F32)
+            for u in range(2):
+                nc.tensor.transpose(vt_ps[:, u, :], val_words[:, block(u)], ident_f32[:])
+            nc.scalar.copy(
+                out=live["val_grouped", b][:, block(BY_ROWS), :].bitcast(F32),
+                in_=vt_ps[:].rearrange("p u c -> p c u"),
             )
 
         def quantise_values(b):
@@ -180,24 +213,24 @@ def tile_mvpam_module_mask_cascade_pb_t_kernel(tc, x, out1, q, k, wv2, bv2, gamm
                 e_words = live["e_rows", b, 2 * pair + a][:].bitcast(F32)
                 for u in range(2):
                     nc.tensor.transpose(et_ps[:, a, u, :], e_words[:, block(u)], ident_f32[:])
-            e_grouped = two.tile([P, 2, P, PACK], BF16, align_bytes=64)
-            nc.scalar.copy(
-                out=e_grouped[:].bitcast(F32), in_=et_ps[:].rearrange("p a u m -> p a m u")
-            )
-            live["e_grouped", b, pair] = e_grouped
-
-        def quantise_e(b, pair):
             if pair == 0:
-                e_codes = two.tile([P, N], U32, align_bytes=64)
-                e_scales = two.tile([P, N], U8, align_bytes=64)
-                live["e_codes", b] = e_codes
-                live["e_scales", b] = e_scales
-            queries = slice(pair * 2 * P, (pair + 1) * 2 * P)
-            nc.vector.quantize_mx(
-                out=live["e_codes", b][:, queries].bitcast(FP8X4),
-                scales=live["e_scales", b][:, queries],
-                in_=live["e_grouped", b, pair][:].rearrange("p a m t -> p (a m t)"),
+                e_grouped = two.tile([P, TILES, P, PACK], BF16, align_bytes=64)
+                live["e_grouped", b] = e_grouped
+            nc.scalar.copy(
+                out=live["e_grouped", b][:, 2 * pair : 2 * pair + 2].bitcast(F32),
+                in_=et_ps[:].rearrange("p a u m -> p a m u"),
             )
+
+        def quantise_e(b):
+            e_codes = two.tile([P, N], U32, align_bytes=64)
+            e_scales = two.tile([P, N], U8, align_bytes=64)
+            nc.vector.quantize_mx(
+                out=e_codes[:].bitcast(FP8X4),
+                scales=e_scales[:],
+                in_=live["e_grouped", b][:].rearrange("p mt m t -> p (mt m t)"),
+            )
+            live["e_codes", b] = e_codes
+            live["e_scales", b] = e_scales
 
         def spread_factors(b):
             factors_ps = ps_turned.tile([P, TILES, P], F32, tag="turned")
@@ -238,7 +271,8 @@ def tile_mvpam_module_mask_cascade_pb_t_kernel(tc, x, out1, q, k, wv2, bv2, gamm
             )
 
         def add_residual(b, ct):
-            nc.gpsimd.tensor_tensor(
+            adder = nc.vector if b == BATCH - 1 and ct % 2 == 1 else nc.gpsimd
+            adder.tensor_tensor(
                 out=live["result", b][:, ct, :],
                 in0=live["result", b][:, ct, :],
                 in1=live["x_rows", b][:, ct, :],
@@ -250,15 +284,17 @@ def tile_mvpam_module_mask_cascade_pb_t_kernel(tc, x, out1, q, k, wv2, bv2, gamm
         w_codes = const.tile([P, C], U32, align_bytes=64)
         w_scales = const.tile([P, C], U8, align_bytes=64)
         gamma_col = const.tile([P, 1], F32)
+        bias_col = const.tile([P, 1], F32)
 
         def prepare_weights():
             for ct in range(TILES):
-                wt_ps = ps_turned.tile([P, PACK, P], BF16, tag="turned")
-                every_fourth = w_rows[:, ct, :].rearrange("c (p j) -> c j p", j=PACK)
-                for j in range(PACK):
-                    nc.tensor.transpose(wt_ps[:, j, :], every_fourth[:, j, :], ident_bf[:])
+                wt_ps = ps_turned.tile([P, 2, P], F32, tag="turned")
+                every_second = w_rows[:, ct, :].bitcast(F32).rearrange("c (p v) -> c v p", v=2)
+                for v in range(2):
+                    nc.tensor.transpose(wt_ps[:, v, :], every_second[:, v, :], ident_f32[:])
                 nc.scalar.copy(
-                    out=w_grouped[:, block(ct), :], in_=wt_ps[:].rearrange("p j c -> p c j")
+                    out=w_grouped[:, block(ct), :].bitcast(F32),
+                    in_=wt_ps[:].rearrange("p v c -> p c v"),
                 )
             nc.vector.quantize_mx(
                 out=w_codes[:].bitcast(FP8X4),
@@ -266,6 +302,9 @@ def tile_mvpam_module_mask_cascade_pb_t_kernel(tc, x, out1, q, k, wv2, bv2, gamm
                 in_=w_grouped[:].rearrange("p c j -> p (c j)"),
             )
             nc.vector.tensor_copy(out=gamma_col[:], in_=gamma_bf[:])
+            bias_ps = ps_turned.tile([P, P], BF16, tag="turned")
+            nc.tensor.transpose(bias_ps[:], bias_rows[:, block(BY_ROWS)], ident_bf[:])
+            nc.scalar.copy(out=bias_col[:], in_=bias_ps[:, 0:1])
 
         def for_tile(stage, step):
             if 0 <= step < STEPS:
@@ -281,6 +320,8 @@ def tile_mvpam_module_mask_cascade_pb_t_kernel(tc, x, out1, q, k, wv2, bv2, gamm
 
         for i in range(-14, STEPS + 8):
             for_batch(load_features, i + 14)
+            if i == -14:
+                nc.sync.dma_start(out=w_rows[:], in_=wv2.rearrange("(ct p) ci -> p ct ci", p=P))
             for_batch(load_queries_keys, i + 10)
             for_batch(load_residual, i)
             if i == -5:
@@ -288,15 +329,17 @@ def tile_mvpam_module_mask_cascade_pb_t_kernel(tc, x, out1, q, k, wv2, bv2, gamm
             for_tile(scores, i + 1)
             for_tile(scale, i - 7)
             for_tile(add_residual, i - 7)
-            for_pair(quantise_e, i - 3)
-            for_batch(quantise_values, i - 2)
+            for_batch(quantise_e, i - 5)
+            for_batch(quantise_values, i - 3)
             for_batch(quantise_features, i + 4)
             for_batch(invert_row_sums, i - 4)
             for_tile(row_maximum, i + 1)
             for_tile(exponentials, i)
             for_tile(values, i + 3)
+            for_batch(value_rows, i + 1)
             for_tile(attend, i - 6)
             for_tile(regroup_features, i + 8)
             for_pair(keys_to_partitions, i - 2)
+            for_batch(rows_to_keys, i)
             for_batch(transpose_queries, i + 5)
             for_batch(spread_factors, i - 5)

@@ -78,8 +78,10 @@ def tile_mvpam_module_mask_cascade_pb_t_kernel(tc, x, out1, q, k, wv2, bv2, gamm
             if nt == 0:
                 feat_grouped = two.tile([P, N, PACK], BF16, align_bytes=64)
                 live["feat_grouped", b] = feat_grouped
-            grouped = live["feat_grouped", b][:, block(nt), :]
-            rows = live["feat_rows", b][:, :, block(nt)].rearrange("p j n -> p n j")
+            grouped = live["feat_grouped", b][:, block(nt), :].rearrange(
+                "p (c i) j -> p c j i", i=4
+            )
+            rows = live["feat_rows", b][:, :, block(nt)].rearrange("p j (c i) -> p c j i", i=4)
             if b == 0:
                 nc.vector.tensor_copy(out=grouped, in_=rows)
             else:

@@ -20,7 +20,6 @@ P = 128
 PACK = 4
 TILES = N // P
 STEPS = BATCH * TILES
-BY_ROWS = 2
 
 FLOPS = 2 * BATCH * (C * C * N + N * N * D + C * N * N)
 
@@ -36,10 +35,9 @@ def tile_mvpam_module_mask_cascade_pb_t_kernel(tc, x, out1, q, k, wv2, bv2, gamm
         two = ctx.enter_context(tc.tile_pool(name="two", bufs=2))
         three = ctx.enter_context(tc.tile_pool(name="three", bufs=3))
         four = ctx.enter_context(tc.tile_pool(name="four", bufs=4))
-        ps_scores = ctx.enter_context(tc.psum_pool(name="ps_scores", bufs=2))
+        ps_scores = ctx.enter_context(tc.psum_pool(name="ps_scores", bufs=3))
         ps_turned = ctx.enter_context(tc.psum_pool(name="ps_turned", bufs=2))
-        ps_att = ctx.enter_context(tc.psum_pool(name="ps_att", bufs=2))
-        ps_quarters = ctx.enter_context(tc.psum_pool(name="ps_quarters", bufs=2))
+        ps_mx = ctx.enter_context(tc.psum_pool(name="ps_mx", bufs=3))
         ctx.enter_context(tc.manual_schedule())
 
         live = {}
@@ -74,18 +72,15 @@ def tile_mvpam_module_mask_cascade_pb_t_kernel(tc, x, out1, q, k, wv2, bv2, gamm
             result = three.tile([P, TILES, N], F32)
             live["result", b] = result
 
-        def regroup_features(b, nt):
-            if nt == 0:
+        def regroup_features(b, half):
+            if half == 0:
                 feat_grouped = two.tile([P, N, PACK], BF16, align_bytes=64)
                 live["feat_grouped", b] = feat_grouped
-            grouped = live["feat_grouped", b][:, block(nt), :].rearrange(
-                "p (c i) j -> p c j i", i=4
+            keys = slice(half * 2 * P, (half + 1) * 2 * P)
+            nc.vector.tensor_copy(
+                out=live["feat_grouped", b][:, keys, :].rearrange("p (c i) j -> p c j i", i=4),
+                in_=live["feat_rows", b][:, :, keys].rearrange("p j (c i) -> p c j i", i=4),
             )
-            rows = live["feat_rows", b][:, :, block(nt)].rearrange("p j (c i) -> p c j i", i=4)
-            if b == 0:
-                nc.vector.tensor_copy(out=grouped, in_=rows)
-            else:
-                nc.scalar.copy(out=grouped, in_=rows)
 
         def quantise_features(b):
             feat_codes = two.tile([P, N], U32, align_bytes=64)
@@ -97,59 +92,45 @@ def tile_mvpam_module_mask_cascade_pb_t_kernel(tc, x, out1, q, k, wv2, bv2, gamm
             )
             live["feat_codes", b] = feat_codes
             live["feat_scales", b] = feat_scales
-            val_grouped = two.tile([P, C, PACK], BF16, align_bytes=64)
-            live["val_grouped", b] = val_grouped
 
-        def values(b, ct):
-            if ct == BY_ROWS:
-                return
-            val_ps = ps_quarters.tile([P, PACK, P], F32, tag="quarters")
-            for t in range(PACK):
-                nc.tensor.matmul_mx(
-                    out=val_ps[:, t, :],
-                    lhsT=live["feat_codes", b][:, block(t)].bitcast(FP8X4),
-                    lhsT_scale=live["feat_scales", b][:, block(t)],
-                    rhs=w_codes[:, block(ct)].bitcast(FP8X4),
-                    rhs_scale=w_scales[:, block(ct)],
-                    start=True,
-                    stop=True,
-                )
-            nc.vector.tensor_tensor(
-                out=live["val_grouped", b][:, block(ct), :],
-                in0=val_ps[:].rearrange("p t c -> p c t"),
-                in1=bias_rows[:, block(ct)].unsqueeze(2).to_broadcast([P, P, PACK]),
-                op=ALU.add,
-            )
-
-        def value_rows(b):
-            val_ps = ps_quarters.tile([P, N], F32, tag="quarters")
+        def value_rows(b, ct):
+            val_ps = ps_mx.tile([P, N], F32, tag="mx")
             nc.tensor.matmul_mx(
                 out=val_ps[:],
-                lhsT=w_codes[:, block(BY_ROWS)].bitcast(FP8X4),
-                lhsT_scale=w_scales[:, block(BY_ROWS)],
+                lhsT=w_codes[:, block(ct)].bitcast(FP8X4),
+                lhsT_scale=w_scales[:, block(ct)],
                 rhs=live["feat_codes", b][:].bitcast(FP8X4),
                 rhs_scale=live["feat_scales", b][:],
                 start=True,
                 stop=True,
             )
-            val_rows = two.tile([P, N], BF16)
+            val_rows = four.tile([P, N], BF16)
             nc.scalar.activation(
-                out=val_rows[:].rearrange("p (u w e) -> p u w e", u=2, e=2),
-                in_=val_ps[:].rearrange("p (u e w) -> p u w e", u=2, e=2),
+                out=val_rows[:],
+                in_=val_ps[:],
                 func=ACT.Identity,
-                bias=bias_col[:],
+                bias=bias_cols[:, ct : ct + 1],
                 scale=1.0,
             )
-            live["val_rows", b] = val_rows
+            live["val_rows", b, ct] = val_rows
 
-        def rows_to_keys(b):
-            vt_ps = ps_turned.tile([P, 2, P], F32, tag="turned")
-            val_words = live["val_rows", b][:].bitcast(F32)
-            for u in range(2):
-                nc.tensor.transpose(vt_ps[:, u, :], val_words[:, block(u)], ident_f32[:])
+        def keys_to_partitions(rows, grouped):
+            turned_ps = ps_turned.tile([P, 2, 2, P], F32, tag="turned")
+            for a in range(2):
+                words = rows[a][:].bitcast(F32)
+                for u in range(2):
+                    nc.tensor.transpose(turned_ps[:, a, u, :], words[:, block(u)], ident_f32[:])
             nc.scalar.copy(
-                out=live["val_grouped", b][:, block(BY_ROWS), :].bitcast(F32),
-                in_=vt_ps[:].rearrange("p u c -> p c u"),
+                out=grouped.bitcast(F32), in_=turned_ps[:].rearrange("p a u r -> p a r u")
+            )
+
+        def turn_values(b, pair):
+            if pair == 0:
+                val_grouped = two.tile([P, TILES, P, PACK], BF16, align_bytes=64)
+                live["val_grouped", b] = val_grouped
+            keys_to_partitions(
+                [live["val_rows", b, 2 * pair + a] for a in range(2)],
+                live["val_grouped", b][:, 2 * pair : 2 * pair + 2],
             )
 
         def quantise_values(b):
@@ -158,7 +139,7 @@ def tile_mvpam_module_mask_cascade_pb_t_kernel(tc, x, out1, q, k, wv2, bv2, gamm
             nc.vector.quantize_mx(
                 out=val_codes[:].bitcast(FP8X4),
                 scales=val_scales[:],
-                in_=live["val_grouped", b][:].rearrange("p c t -> p (c t)"),
+                in_=live["val_grouped", b][:].rearrange("p ct c t -> p (ct c t)"),
             )
             live["val_codes", b] = val_codes
             live["val_scales", b] = val_scales
@@ -168,7 +149,7 @@ def tile_mvpam_module_mask_cascade_pb_t_kernel(tc, x, out1, q, k, wv2, bv2, gamm
             for mt in range(TILES):
                 nc.tensor.transpose(qt_ps[:, mt, :], live["q_rows", b][:, mt, :], ident_bf[:])
             q_turned = two.tile([P, N], BF16)
-            nc.scalar.copy(out=q_turned[:], in_=qt_ps[:].rearrange("d mt m -> d (mt m)"))
+            nc.vector.tensor_copy(out=q_turned[:], in_=qt_ps[:].rearrange("d mt m -> d (mt m)"))
             live["q_turned", b] = q_turned
 
         def scores(b, mt):
@@ -195,8 +176,8 @@ def tile_mvpam_module_mask_cascade_pb_t_kernel(tc, x, out1, q, k, wv2, bv2, gamm
                 live["row_sums", b] = row_sums
             e_rows = four.tile([P, N], BF16)
             nc.scalar.activation(
-                out=e_rows[:].rearrange("p (u w e) -> p u w e", u=2, e=2),
-                in_=live["s_ps", b, mt][:].rearrange("p (u e w) -> p u w e", u=2, e=2),
+                out=e_rows[:],
+                in_=live["s_ps", b, mt][:],
                 func=ACT.Exp,
                 bias=live["neg_max", b, mt][:],
                 scale=1.0,
@@ -209,18 +190,13 @@ def tile_mvpam_module_mask_cascade_pb_t_kernel(tc, x, out1, q, k, wv2, bv2, gamm
             nc.vector.reciprocal(out=inv_sums[:], in_=live["row_sums", b][:])
             live["inv_sums", b] = inv_sums
 
-        def keys_to_partitions(b, pair):
-            et_ps = ps_turned.tile([P, 2, 2, P], F32, tag="turned")
-            for a in range(2):
-                e_words = live["e_rows", b, 2 * pair + a][:].bitcast(F32)
-                for u in range(2):
-                    nc.tensor.transpose(et_ps[:, a, u, :], e_words[:, block(u)], ident_f32[:])
+        def turn_e(b, pair):
             if pair == 0:
                 e_grouped = two.tile([P, TILES, P, PACK], BF16, align_bytes=64)
                 live["e_grouped", b] = e_grouped
-            nc.scalar.copy(
-                out=live["e_grouped", b][:, 2 * pair : 2 * pair + 2].bitcast(F32),
-                in_=et_ps[:].rearrange("p a u m -> p a m u"),
+            keys_to_partitions(
+                [live["e_rows", b, 2 * pair + a] for a in range(2)],
+                live["e_grouped", b][:, 2 * pair : 2 * pair + 2],
             )
 
         def quantise_e(b):
@@ -252,7 +228,7 @@ def tile_mvpam_module_mask_cascade_pb_t_kernel(tc, x, out1, q, k, wv2, bv2, gamm
             live["factors", b] = factors
 
         def attend(b, ct):
-            att_ps = ps_att.tile([P, N], F32)
+            att_ps = ps_mx.tile([P, N], F32, tag="mx")
             nc.tensor.matmul_mx(
                 out=att_ps[:],
                 lhsT=live["val_codes", b][:, block(ct)].bitcast(FP8X4),
@@ -286,7 +262,7 @@ def tile_mvpam_module_mask_cascade_pb_t_kernel(tc, x, out1, q, k, wv2, bv2, gamm
         w_codes = const.tile([P, C], U32, align_bytes=64)
         w_scales = const.tile([P, C], U8, align_bytes=64)
         gamma_col = const.tile([P, 1], F32)
-        bias_col = const.tile([P, 1], F32)
+        bias_cols = const.tile([P, TILES], F32)
 
         def prepare_weights():
             for ct in range(TILES):
@@ -304,9 +280,10 @@ def tile_mvpam_module_mask_cascade_pb_t_kernel(tc, x, out1, q, k, wv2, bv2, gamm
                 in_=w_grouped[:].rearrange("p c j -> p (c j)"),
             )
             nc.vector.tensor_copy(out=gamma_col[:], in_=gamma_bf[:])
-            bias_ps = ps_turned.tile([P, P], BF16, tag="turned")
-            nc.tensor.transpose(bias_ps[:], bias_rows[:, block(BY_ROWS)], ident_bf[:])
-            nc.scalar.copy(out=bias_col[:], in_=bias_ps[:, 0:1])
+            bias_ps = ps_turned.tile([P, TILES, P], BF16, tag="turned")
+            for ct in range(TILES):
+                nc.tensor.transpose(bias_ps[:, ct, :], bias_rows[:, block(ct)], ident_bf[:])
+            nc.scalar.copy(out=bias_cols[:], in_=bias_ps[:, :, 0])
 
         def for_tile(stage, step):
             if 0 <= step < STEPS:
@@ -326,22 +303,21 @@ def tile_mvpam_module_mask_cascade_pb_t_kernel(tc, x, out1, q, k, wv2, bv2, gamm
                 nc.sync.dma_start(out=w_rows[:], in_=wv2.rearrange("(ct p) ci -> p ct ci", p=P))
             for_batch(load_queries_keys, i + 10)
             for_batch(load_residual, i)
-            if i == -5:
+            if i == -4:
                 prepare_weights()
             for_tile(scores, i + 1)
             for_tile(scale, i - 7)
             for_tile(add_residual, i - 7)
+            for_pair(regroup_features, i + 8)
             for_batch(quantise_e, i - 5)
-            for_batch(quantise_values, i - 3)
-            for_batch(quantise_features, i + 4)
+            for_batch(quantise_values, i - 2)
+            for_batch(quantise_features, i + 5)
             for_batch(invert_row_sums, i - 4)
             for_tile(row_maximum, i + 1)
             for_tile(exponentials, i)
-            for_tile(values, i + 3)
-            for_batch(value_rows, i + 1)
+            for_tile(value_rows, i + 3)
             for_tile(attend, i - 6)
-            for_tile(regroup_features, i + 8)
-            for_pair(keys_to_partitions, i - 2)
-            for_batch(rows_to_keys, i)
+            for_pair(turn_e, i - 2)
+            for_pair(turn_values, i + 1)
             for_batch(transpose_queries, i + 5)
             for_batch(spread_factors, i - 5)

@@ -72,15 +72,13 @@ def tile_mvpam_module_mask_cascade_pb_t_kernel(tc, x, out1, q, k, wv2, bv2, gamm
             result = three.tile([P, TILES, N], F32)
             live["result", b] = result
 
-        def regroup_features(b, half):
-            if half == 0:
-                feat_grouped = two.tile([P, N, PACK], BF16, align_bytes=64)
-                live["feat_grouped", b] = feat_grouped
-            keys = slice(half * 2 * P, (half + 1) * 2 * P)
+        def regroup_features(b):
+            feat_grouped = two.tile([P, N, PACK], BF16, align_bytes=64)
             nc.vector.tensor_copy(
-                out=live["feat_grouped", b][:, keys, :].rearrange("p (c i) j -> p c j i", i=4),
-                in_=live["feat_rows", b][:, :, keys].rearrange("p j (c i) -> p c j i", i=4),
+                out=feat_grouped[:].rearrange("p (c i) j -> p c j i", i=4),
+                in_=live["feat_rows", b][:].rearrange("p j (c i) -> p c j i", i=4),
             )
+            live["feat_grouped", b] = feat_grouped
 
         def quantise_features(b):
             feat_codes = two.tile([P, N], U32, align_bytes=64)
@@ -149,7 +147,7 @@ def tile_mvpam_module_mask_cascade_pb_t_kernel(tc, x, out1, q, k, wv2, bv2, gamm
             for mt in range(TILES):
                 nc.tensor.transpose(qt_ps[:, mt, :], live["q_rows", b][:, mt, :], ident_bf[:])
             q_turned = two.tile([P, N], BF16)
-            nc.vector.tensor_copy(out=q_turned[:], in_=qt_ps[:].rearrange("d mt m -> d (mt m)"))
+            nc.scalar.copy(out=q_turned[:], in_=qt_ps[:].rearrange("d mt m -> d (mt m)"))
             live["q_turned", b] = q_turned
 
         def scores(b, mt):
@@ -297,21 +295,21 @@ def tile_mvpam_module_mask_cascade_pb_t_kernel(tc, x, out1, q, k, wv2, bv2, gamm
             if 0 <= step < STEPS and step % TILES == 0:
                 stage(step // TILES)
 
-        for i in range(-14, STEPS + 8):
-            for_batch(load_features, i + 14)
-            if i == -14:
+        for i in range(-12, STEPS + 8):
+            for_batch(load_features, i + 12)
+            if i == -12:
                 nc.sync.dma_start(out=w_rows[:], in_=wv2.rearrange("(ct p) ci -> p ct ci", p=P))
-            for_batch(load_queries_keys, i + 10)
+            for_batch(load_queries_keys, i + 9)
             for_batch(load_residual, i)
-            if i == -4:
-                prepare_weights()
             for_tile(scores, i + 1)
             for_tile(scale, i - 7)
             for_tile(add_residual, i - 7)
-            for_pair(regroup_features, i + 8)
+            for_batch(regroup_features, i + 8)
             for_batch(quantise_e, i - 5)
             for_batch(quantise_values, i - 2)
             for_batch(quantise_features, i + 5)
+            if i == -5:
+                prepare_weights()
             for_batch(invert_row_sums, i - 4)
             for_tile(row_maximum, i + 1)
             for_tile(exponentials, i)

@@ -20,6 +20,7 @@ P = 128
 PACK = 4
 TILES = N // P
 STEPS = BATCH * TILES
+LAST = BATCH - 1
 
 FLOPS = 2 * BATCH * (C * C * N + N * N * D + C * N * N)
 
@@ -35,6 +36,7 @@ def tile_mvpam_module_mask_cascade_pb_t_kernel(tc, x, out1, q, k, wv2, bv2, gamm
         two = ctx.enter_context(tc.tile_pool(name="two", bufs=2))
         three = ctx.enter_context(tc.tile_pool(name="three", bufs=3))
         four = ctx.enter_context(tc.tile_pool(name="four", bufs=4))
+        results = ctx.enter_context(tc.tile_pool(name="results", bufs=BATCH))
         ps_scores = ctx.enter_context(tc.psum_pool(name="ps_scores", bufs=3))
         ps_turned = ctx.enter_context(tc.psum_pool(name="ps_turned", bufs=2))
         ps_mx = ctx.enter_context(tc.psum_pool(name="ps_mx", bufs=3))
@@ -51,6 +53,10 @@ def tile_mvpam_module_mask_cascade_pb_t_kernel(tc, x, out1, q, k, wv2, bv2, gamm
         make_identity(nc, ident_bf[:])
         ident_f32 = const.tile([P, P], F32)
         make_identity(nc, ident_f32[:])
+
+        neg_max = const.tile([P, BATCH, TILES], F32)
+        row_sums = const.tile([P, BATCH, TILES], F32)
+        inv_sums = const.tile([P, BATCH, TILES], F32)
 
         def load_features(b):
             feat_rows = three.tile([P, PACK, N], BF16)
@@ -69,7 +75,7 @@ def tile_mvpam_module_mask_cascade_pb_t_kernel(tc, x, out1, q, k, wv2, bv2, gamm
             x_rows = three.tile([P, TILES, N], BF16)
             nc.sync.dma_start(out=x_rows[:], in_=x[b].rearrange("(ct p) m -> p ct m", p=P))
             live["x_rows", b] = x_rows
-            result = three.tile([P, TILES, N], F32)
+            result = results.tile([P, TILES, N], F32)
             live["result", b] = result
 
         def regroup_features(b):
@@ -147,7 +153,11 @@ def tile_mvpam_module_mask_cascade_pb_t_kernel(tc, x, out1, q, k, wv2, bv2, gamm
             for mt in range(TILES):
                 nc.tensor.transpose(qt_ps[:, mt, :], live["q_rows", b][:, mt, :], ident_bf[:])
             q_turned = two.tile([P, N], BF16)
-            nc.scalar.copy(out=q_turned[:], in_=qt_ps[:].rearrange("d mt m -> d (mt m)"))
+            turned = qt_ps[:].rearrange("d mt m -> d (mt m)")
+            if b % 2 == 0:
+                nc.scalar.copy(out=q_turned[:], in_=turned)
+            else:
+                nc.vector.tensor_copy(out=q_turned[:], in_=turned)
             live["q_turned", b] = q_turned
 
         def scores(b, mt):
@@ -162,31 +172,34 @@ def tile_mvpam_module_mask_cascade_pb_t_kernel(tc, x, out1, q, k, wv2, bv2, gamm
             live["s_ps", b, mt] = s_ps
 
         def row_maximum(b, mt):
-            neg_max = three.tile([P, 1], F32)
             nc.vector.tensor_reduce(
-                out=neg_max[:], in_=live["s_ps", b, mt][:], axis=AXIS.X, op=ALU.max, negate=True
+                out=neg_max[:, b, mt : mt + 1],
+                in_=live["s_ps", b, mt][:],
+                axis=AXIS.X,
+                op=ALU.max,
+                negate=True,
             )
-            live["neg_max", b, mt] = neg_max
 
         def exponentials(b, mt):
-            if mt == 0:
-                row_sums = three.tile([P, TILES], F32)
-                live["row_sums", b] = row_sums
             e_rows = four.tile([P, N], BF16)
             nc.scalar.activation(
                 out=e_rows[:],
                 in_=live["s_ps", b, mt][:],
                 func=ACT.Exp,
-                bias=live["neg_max", b, mt][:],
+                bias=neg_max[:, b, mt : mt + 1],
                 scale=1.0,
-                accum_out=live["row_sums", b][:, mt : mt + 1],
+                accum_out=row_sums[:, b, mt : mt + 1],
             )
             live["e_rows", b, mt] = e_rows
 
-        def invert_row_sums(b):
-            inv_sums = three.tile([P, TILES], F32)
-            nc.vector.reciprocal(out=inv_sums[:], in_=live["row_sums", b][:])
-            live["inv_sums", b] = inv_sums
+        def ready_tiles(b, pair):
+            return (2 * pair, 2 * pair + 2) if b == LAST else (0, TILES)
+
+        def invert_row_sums(b, pair):
+            if b < LAST and pair == 0:
+                return
+            first, end = ready_tiles(b, pair)
+            nc.vector.reciprocal(out=inv_sums[:, b, first:end], in_=row_sums[:, b, first:end])
 
         def turn_e(b, pair):
             if pair == 0:
@@ -197,23 +210,27 @@ def tile_mvpam_module_mask_cascade_pb_t_kernel(tc, x, out1, q, k, wv2, bv2, gamm
                 live["e_grouped", b][:, 2 * pair : 2 * pair + 2],
             )
 
-        def quantise_e(b):
-            e_codes = two.tile([P, N], U32, align_bytes=64)
-            e_scales = two.tile([P, N], U8, align_bytes=64)
+        def quantise_e(b, pair):
+            if b < LAST and pair == 0:
+                return
+            first, end = ready_tiles(b, pair)
+            if first == 0:
+                e_codes = two.tile([P, N], U32, align_bytes=64)
+                e_scales = two.tile([P, N], U8, align_bytes=64)
+                live["e_codes", b] = e_codes
+                live["e_scales", b] = e_scales
             nc.vector.quantize_mx(
-                out=e_codes[:].bitcast(FP8X4),
-                scales=e_scales[:],
-                in_=live["e_grouped", b][:].rearrange("p mt m t -> p (mt m t)"),
+                out=live["e_codes", b][:, first * P : end * P].bitcast(FP8X4),
+                scales=live["e_scales", b][:, first * P : end * P],
+                in_=live["e_grouped", b][:, first:end].rearrange("p mt m t -> p (mt m t)"),
             )
-            live["e_codes", b] = e_codes
-            live["e_scales", b] = e_scales
 
         def spread_factors(b):
             factors_ps = ps_turned.tile([P, TILES, P], F32, tag="turned")
             for mt in range(TILES):
                 nc.tensor.transpose(
                     factors_ps[:, mt, :],
-                    live["inv_sums", b][:, mt : mt + 1].to_broadcast([P, P]),
+                    inv_sums[:, b, mt : mt + 1].to_broadcast([P, P]),
                     ident_f32[:],
                 )
             factors = two.tile([P, N], F32)
@@ -247,7 +264,7 @@ def tile_mvpam_module_mask_cascade_pb_t_kernel(tc, x, out1, q, k, wv2, bv2, gamm
             )
 
         def add_residual(b, ct):
-            adder = nc.vector if b == BATCH - 1 and ct % 2 == 1 else nc.gpsimd
+            adder = nc.vector if b == LAST - 1 and ct >= 3 else nc.gpsimd
             adder.tensor_tensor(
                 out=live["result", b][:, ct, :],
                 in0=live["result", b][:, ct, :],
@@ -255,6 +272,45 @@ def tile_mvpam_module_mask_cascade_pb_t_kernel(tc, x, out1, q, k, wv2, bv2, gamm
                 op=ALU.add,
             )
             nc.sync.dma_start(out=out[b, block(ct), :], in_=live["result", b][:, ct, :])
+
+        def attend_rows(b, mt):
+            att_ps = ps_mx.tile([P, C], F32, tag="mx")
+            nc.tensor.matmul_mx(
+                out=att_ps[:],
+                lhsT=live["e_codes", b][:, block(mt)].bitcast(FP8X4),
+                lhsT_scale=live["e_scales", b][:, block(mt)],
+                rhs=live["val_codes", b][:].bitcast(FP8X4),
+                rhs_scale=live["val_scales", b][:],
+                start=True,
+                stop=True,
+            )
+            att_rows = four.tile([P, C], F32)
+            nc.scalar.activation(
+                out=att_rows[:],
+                in_=att_ps[:],
+                func=ACT.Copy,
+                scale=inv_sums[:, b, mt : mt + 1],
+            )
+            live["att_rows", b, mt] = att_rows
+
+        def finish_rows(b, mt):
+            result_ps = ps_mx.tile([P, TILES, P], F32, tag="mx")
+            for ct in range(TILES):
+                nc.tensor.transpose(
+                    result_ps[:, ct, :], live["att_rows", b, mt][:, block(ct)], ident_f32[:]
+                )
+            nc.vector.scalar_tensor_tensor(
+                out=live["result", b][:, :, block(mt)],
+                in0=result_ps[:],
+                scalar=gamma_col[:],
+                in1=live["x_rows", b][:, :, block(mt)],
+                op0=ALU.mult,
+                op1=ALU.add,
+            )
+            nc.sync.dma_start(
+                out=out[b].rearrange("(ct p) m -> p ct m", p=P)[:, :, block(mt)],
+                in_=live["result", b][:, :, block(mt)],
+            )
 
         w_grouped = const.tile([P, C, PACK], BF16, align_bytes=64)
         w_codes = const.tile([P, C], U32, align_bytes=64)
@@ -295,6 +351,15 @@ def tile_mvpam_module_mask_cascade_pb_t_kernel(tc, x, out1, q, k, wv2, bv2, gamm
             if 0 <= step < STEPS and step % TILES == 0:
                 stage(step // TILES)
 
+        def but_last(stage, step):
+            if step < LAST * TILES:
+                for_tile(stage, step)
+
+        def for_last_pair(stage, step):
+            if LAST * TILES <= step < STEPS and step % 2 == 0:
+                for u in range(2):
+                    stage(LAST, step % TILES + u)
+
         for i in range(-12, STEPS + 8):
             for_batch(load_features, i + 12)
             if i == -12:
@@ -302,20 +367,23 @@ def tile_mvpam_module_mask_cascade_pb_t_kernel(tc, x, out1, q, k, wv2, bv2, gamm
             for_batch(load_queries_keys, i + 9)
             for_batch(load_residual, i)
             for_tile(scores, i + 1)
-            for_tile(scale, i - 7)
-            for_tile(add_residual, i - 7)
+            but_last(scale, i - 7)
+            but_last(add_residual, i - 7)
             for_batch(regroup_features, i + 8)
-            for_batch(quantise_e, i - 5)
+            for_pair(quantise_e, i - 3)
             for_batch(quantise_values, i - 2)
             for_batch(quantise_features, i + 5)
             if i == -5:
                 prepare_weights()
-            for_batch(invert_row_sums, i - 4)
+            for_pair(invert_row_sums, i - 2)
             for_tile(row_maximum, i + 1)
-            for_tile(exponentials, i)
             for_tile(value_rows, i + 3)
-            for_tile(attend, i - 6)
+            but_last(attend, i - 6)
             for_pair(turn_e, i - 2)
             for_pair(turn_values, i + 1)
+            for_tile(exponentials, i)
             for_batch(transpose_queries, i + 5)
-            for_batch(spread_factors, i - 5)
+            if i - 5 < LAST * TILES:
+                for_batch(spread_factors, i - 5)
+            for_last_pair(attend_rows, i - 4)
+            for_last_pair(finish_rows, i - 6)

@@ -45,10 +45,9 @@ def tile_mvpam_module_mask_cascade_pb_t_kernel(tc, x, out1, q, k, wv2, bv2, gamm
         live = {}
 
         w_rows = const.tile([P, TILES, C], BF16)
-        bias_rows = const.tile([P, C], BF16)
-        nc.scalar.dma_start(out=bias_rows[:], in_=bv2.partition_broadcast(P))
+        bias_row = const.tile([P, C], BF16)
+        nc.vector.memset(bias_row[:], 0.0)
         gamma_bf = const.tile([P, 1], BF16)
-        nc.scalar.dma_start(out=gamma_bf[:], in_=gamma.partition_broadcast(P))
         ident_bf = const.tile([P, P], BF16)
         make_identity(nc, ident_bf[:])
         ident_f32 = const.tile([P, P], F32)
@@ -336,7 +335,7 @@ def tile_mvpam_module_mask_cascade_pb_t_kernel(tc, x, out1, q, k, wv2, bv2, gamm
             nc.vector.tensor_copy(out=gamma_col[:], in_=gamma_bf[:])
             bias_ps = ps_turned.tile([P, TILES, P], BF16, tag="turned")
             for ct in range(TILES):
-                nc.tensor.transpose(bias_ps[:, ct, :], bias_rows[:, block(ct)], ident_bf[:])
+                nc.tensor.transpose(bias_ps[:, ct, :], bias_row[:, block(ct)], ident_bf[:])
             nc.scalar.copy(out=bias_cols[:], in_=bias_ps[:, :, 0])
 
         def for_tile(stage, step):
@@ -364,7 +363,10 @@ def tile_mvpam_module_mask_cascade_pb_t_kernel(tc, x, out1, q, k, wv2, bv2, gamm
             for_batch(load_features, i + 12)
             if i == -12:
                 nc.sync.dma_start(out=w_rows[:], in_=wv2.rearrange("(ct p) ci -> p ct ci", p=P))
+                nc.sync.dma_start(out=bias_row[0:1, :], in_=bv2.unsqueeze(0))
             for_batch(load_queries_keys, i + 9)
+            if i == -9:
+                nc.sync.dma_start(out=gamma_bf[:], in_=gamma.partition_broadcast(P))
             for_batch(load_residual, i)
             for_tile(scores, i + 1)
             but_last(scale, i - 7)

from contextlib import ExitStack

import concourse.mybir as mybir
from concourse.masks import make_identity

F32 = mybir.dt.float32
BF16 = mybir.dt.bfloat16
U32 = mybir.dt.uint32
U8 = mybir.dt.uint8
FP8X4 = mybir.dt.float8_e4m3fn_x4
ALU = mybir.AluOpType
ACT = mybir.ActivationFunctionType
AXIS = mybir.AxisListType

BATCH = 16
C = 512
N = 512
D = 128
P = 128
PACK = 4
TILES = N // P
STEPS = BATCH * TILES
LAST = BATCH - 1

FLOPS = 2 * BATCH * (C * C * N + N * N * D + C * N * N)


def block(i):
    return slice(i * P, (i + 1) * P)


def tile_mvpam_module_mask_cascade_pb_t_kernel(tc, x, out1, q, k, wv2, bv2, gamma, out):
    nc = tc.nc
    with ExitStack() as ctx:
        const = ctx.enter_context(tc.tile_pool(name="const", bufs=1))
        two = ctx.enter_context(tc.tile_pool(name="two", bufs=2))
        three = ctx.enter_context(tc.tile_pool(name="three", bufs=3))
        four = ctx.enter_context(tc.tile_pool(name="four", bufs=4))
        results = ctx.enter_context(tc.tile_pool(name="results", bufs=BATCH))
        ps_scores = ctx.enter_context(tc.psum_pool(name="ps_scores", bufs=3))
        ps_turned = ctx.enter_context(tc.psum_pool(name="ps_turned", bufs=2))
        ps_mx = ctx.enter_context(tc.psum_pool(name="ps_mx", bufs=3))
        ctx.enter_context(tc.manual_schedule())

        live = {}

        w_rows = const.tile([P, TILES, C], BF16)
        bias_row = const.tile([P, C], BF16)
        nc.vector.memset(bias_row[:], 0.0)
        gamma_bf = const.tile([P, 1], BF16)
        ident_bf = const.tile([P, P], BF16)
        make_identity(nc, ident_bf[:])
        ident_f32 = const.tile([P, P], F32)
        make_identity(nc, ident_f32[:])

        neg_max = const.tile([P, BATCH, TILES], F32)
        row_sums = const.tile([P, BATCH, TILES], F32)
        inv_sums = const.tile([P, BATCH, TILES], F32)

        def load_features(b):
            feat_rows = three.tile([P, PACK, N], BF16)
            nc.sync.dma_start(out=feat_rows[:], in_=out1[b].rearrange("(p j) n -> p j n", j=PACK))
            live["feat_rows", b] = feat_rows

        def load_queries_keys(b):
            q_rows = two.tile([P, TILES, D], BF16)
            nc.sync.dma_start(out=q_rows[:], in_=q[b].rearrange("(mt p) d -> p mt d", p=P))
            live["q_rows", b] = q_rows
            k_rows = three.tile([P, N], BF16)
            nc.sync.dma_start(out=k_rows[:], in_=k[b])
            live["k_rows", b] = k_rows

        def load_residual(b):
            x_rows = three.tile([P, TILES, N], BF16)
            nc.sync.dma_start(out=x_rows[:], in_=x[b].rearrange("(ct p) m -> p ct m", p=P))
            live["x_rows", b] = x_rows
            result = results.tile([P, TILES, N], F32)
            live["result", b] = result

        def regroup_features(b):
            feat_grouped = two.tile([P, N, PACK], BF16, align_bytes=64)
            nc.vector.tensor_copy(
                out=feat_grouped[:].rearrange("p (c i) j -> p c j i", i=4),
                in_=live["feat_rows", b][:].rearrange("p j (c i) -> p c j i", i=4),
            )
            live["feat_grouped", b] = feat_grouped

        def quantise_features(b):
            feat_codes = two.tile([P, N], U32, align_bytes=64)
            feat_scales = two.tile([P, N], U8, align_bytes=64)
            nc.vector.quantize_mx(
                out=feat_codes[:].bitcast(FP8X4),
                scales=feat_scales[:],
                in_=live["feat_grouped", b][:].rearrange("p n j -> p (n j)"),
            )
            live["feat_codes", b] = feat_codes
            live["feat_scales", b] = feat_scales

        def value_rows(b, ct):
            val_ps = ps_mx.tile([P, N], F32, tag="mx")
            nc.tensor.matmul_mx(
                out=val_ps[:],
                lhsT=w_codes[:, block(ct)].bitcast(FP8X4),
                lhsT_scale=w_scales[:, block(ct)],
                rhs=live["feat_codes", b][:].bitcast(FP8X4),
                rhs_scale=live["feat_scales", b][:],
                start=True,
                stop=True,
            )
            val_rows = four.tile([P, N], BF16)
            nc.scalar.activation(
                out=val_rows[:],
                in_=val_ps[:],
                func=ACT.Identity,
                bias=bias_cols[:, ct : ct + 1],
                scale=1.0,
            )
            live["val_rows", b, ct] = val_rows

        def keys_to_partitions(rows, grouped):
            turned_ps = ps_turned.tile([P, 2, 2, P], F32, tag="turned")
            for a in range(2):
                words = rows[a][:].bitcast(F32)
                for u in range(2):
                    nc.tensor.transpose(turned_ps[:, a, u, :], words[:, block(u)], ident_f32[:])
            nc.scalar.copy(
                out=grouped.bitcast(F32), in_=turned_ps[:].rearrange("p a u r -> p a r u")
            )

        def turn_values(b, pair):
            if pair == 0:
                val_grouped = two.tile([P, TILES, P, PACK], BF16, align_bytes=64)
                live["val_grouped", b] = val_grouped
            keys_to_partitions(
                [live["val_rows", b, 2 * pair + a] for a in range(2)],
                live["val_grouped", b][:, 2 * pair : 2 * pair + 2],
            )

        def quantise_values(b):
            val_codes = two.tile([P, C], U32, align_bytes=64)
            val_scales = two.tile([P, C], U8, align_bytes=64)
            nc.vector.quantize_mx(
                out=val_codes[:].bitcast(FP8X4),
                scales=val_scales[:],
                in_=live["val_grouped", b][:].rearrange("p ct c t -> p (ct c t)"),
            )
            live["val_codes", b] = val_codes
            live["val_scales", b] = val_scales

        def transpose_queries(b):
            qt_ps = ps_turned.tile([P, TILES, P], BF16, tag="turned")
            for mt in range(TILES):
                nc.tensor.transpose(qt_ps[:, mt, :], live["q_rows", b][:, mt, :], ident_bf[:])
            q_turned = two.tile([P, N], BF16)
            turned = qt_ps[:].rearrange("d mt m -> d (mt m)")
            if b % 2 == 0:
                nc.scalar.copy(out=q_turned[:], in_=turned)
            else:
                nc.vector.tensor_copy(out=q_turned[:], in_=turned)
            live["q_turned", b] = q_turned

        def scores(b, mt):
            s_ps = ps_scores.tile([P, N], F32)
            nc.tensor.matmul(
                out=s_ps[:],
                lhsT=live["q_turned", b][:, block(mt)],
                rhs=live["k_rows", b][:],
                start=True,
                stop=True,
            )
            live["s_ps", b, mt] = s_ps

        def row_maximum(b, mt):
            nc.vector.tensor_reduce(
                out=neg_max[:, b, mt : mt + 1],
                in_=live["s_ps", b, mt][:],
                axis=AXIS.X,
                op=ALU.max,
                negate=True,
            )

        def exponentials(b, mt):
            e_rows = four.tile([P, N], BF16)
            nc.scalar.activation(
                out=e_rows[:],
                in_=live["s_ps", b, mt][:],
                func=ACT.Exp,
                bias=neg_max[:, b, mt : mt + 1],
                scale=1.0,
                accum_out=row_sums[:, b, mt : mt + 1],
            )
            live["e_rows", b, mt] = e_rows

        def ready_tiles(b, pair):
            return (2 * pair, 2 * pair + 2) if b == LAST else (0, TILES)

        def invert_row_sums(b, pair):
            if b < LAST and pair == 0:
                return
            first, end = ready_tiles(b, pair)
            nc.vector.reciprocal(out=inv_sums[:, b, first:end], in_=row_sums[:, b, first:end])

        def turn_e(b, pair):
            if pair == 0:
                e_grouped = two.tile([P, TILES, P, PACK], BF16, align_bytes=64)
                live["e_grouped", b] = e_grouped
            keys_to_partitions(
                [live["e_rows", b, 2 * pair + a] for a in range(2)],
                live["e_grouped", b][:, 2 * pair : 2 * pair + 2],
            )

        def quantise_e(b, pair):
            if b < LAST and pair == 0:
                return
            first, end = ready_tiles(b, pair)
            if first == 0:
                e_codes = two.tile([P, N], U32, align_bytes=64)
                e_scales = two.tile([P, N], U8, align_bytes=64)
                live["e_codes", b] = e_codes
                live["e_scales", b] = e_scales
            nc.vector.quantize_mx(
                out=live["e_codes", b][:, first * P : end * P].bitcast(FP8X4),
                scales=live["e_scales", b][:, first * P : end * P],
                in_=live["e_grouped", b][:, first:end].rearrange("p mt m t -> p (mt m t)"),
            )

        def spread_factors(b):
            factors_ps = ps_turned.tile([P, TILES, P], F32, tag="turned")
            for mt in range(TILES):
                nc.tensor.transpose(
                    factors_ps[:, mt, :],
                    inv_sums[:, b, mt : mt + 1].to_broadcast([P, P]),
                    ident_f32[:],
                )
            factors = two.tile([P, N], F32)
            nc.scalar.activation(
                out=factors[:],
                in_=factors_ps[:].rearrange("p mt m -> p (mt m)"),
                func=ACT.Copy,
                scale=gamma_col[:],
            )
            live["factors", b] = factors

        def attend(b, ct):
            att_ps = ps_mx.tile([P, N], F32, tag="mx")
            nc.tensor.matmul_mx(
                out=att_ps[:],
                lhsT=live["val_codes", b][:, block(ct)].bitcast(FP8X4),
                lhsT_scale=live["val_scales", b][:, block(ct)],
                rhs=live["e_codes", b][:].bitcast(FP8X4),
                rhs_scale=live["e_scales", b][:],
                start=True,
                stop=True,
            )
            live["att_ps", b, ct] = att_ps

        def scale(b, ct):
            nc.vector.tensor_tensor(
                out=live["result", b][:, ct, :],
                in0=live["att_ps", b, ct][:],
                in1=live["factors", b][:],
                op=ALU.mult,
            )

        def add_residual(b, ct):
            adder = nc.vector if b == LAST - 1 and ct >= 3 else nc.gpsimd
            adder.tensor_tensor(
                out=live["result", b][:, ct, :],
                in0=live["result", b][:, ct, :],
                in1=live["x_rows", b][:, ct, :],
                op=ALU.add,
            )
            nc.sync.dma_start(out=out[b, block(ct), :], in_=live["result", b][:, ct, :])

        def attend_rows(b, mt):
            att_ps = ps_mx.tile([P, C], F32, tag="mx")
            nc.tensor.matmul_mx(
                out=att_ps[:],
                lhsT=live["e_codes", b][:, block(mt)].bitcast(FP8X4),
                lhsT_scale=live["e_scales", b][:, block(mt)],
                rhs=live["val_codes", b][:].bitcast(FP8X4),
                rhs_scale=live["val_scales", b][:],
                start=True,
                stop=True,
            )
            att_rows = four.tile([P, C], F32)
            nc.scalar.activation(
                out=att_rows[:],
                in_=att_ps[:],
                func=ACT.Copy,
                scale=inv_sums[:, b, mt : mt + 1],
            )
            live["att_rows", b, mt] = att_rows

        def finish_rows(b, mt):
            result_ps = ps_mx.tile([P, TILES, P], F32, tag="mx")
            for ct in range(TILES):
                nc.tensor.transpose(
                    result_ps[:, ct, :], live["att_rows", b, mt][:, block(ct)], ident_f32[:]
                )
            nc.vector.scalar_tensor_tensor(
                out=live["result", b][:, :, block(mt)],
                in0=result_ps[:],
                scalar=gamma_col[:],
                in1=live["x_rows", b][:, :, block(mt)],
                op0=ALU.mult,
                op1=ALU.add,
            )
            nc.sync.dma_start(
                out=out[b].rearrange("(ct p) m -> p ct m", p=P)[:, :, block(mt)],
                in_=live["result", b][:, :, block(mt)],
            )

        w_grouped = const.tile([P, C, PACK], BF16, align_bytes=64)
        w_codes = const.tile([P, C], U32, align_bytes=64)
        w_scales = const.tile([P, C], U8, align_bytes=64)
        gamma_col = const.tile([P, 1], F32)
        bias_cols = const.tile([P, TILES], F32)

        def prepare_weights():
            for ct in range(TILES):
                wt_ps = ps_turned.tile([P, 2, P], F32, tag="turned")
                every_second = w_rows[:, ct, :].bitcast(F32).rearrange("c (p v) -> c v p", v=2)
                for v in range(2):
                    nc.tensor.transpose(wt_ps[:, v, :], every_second[:, v, :], ident_f32[:])
                nc.scalar.copy(
                    out=w_grouped[:, block(ct), :].bitcast(F32),
                    in_=wt_ps[:].rearrange("p v c -> p c v"),
                )
            nc.vector.quantize_mx(
                out=w_codes[:].bitcast(FP8X4),
                scales=w_scales[:],
                in_=w_grouped[:].rearrange("p c j -> p (c j)"),
            )
            nc.vector.tensor_copy(out=gamma_col[:], in_=gamma_bf[:])
            bias_ps = ps_turned.tile([P, TILES, P], BF16, tag="turned")
            for ct in range(TILES):
                nc.tensor.transpose(bias_ps[:, ct, :], bias_row[:, block(ct)], ident_bf[:])
            nc.scalar.copy(out=bias_cols[:], in_=bias_ps[:, :, 0])

        def for_tile(stage, step):
            if 0 <= step < STEPS:
                stage(*divmod(step, TILES))

        def for_pair(stage, step):
            if 0 <= step < STEPS and step % 2 == 0:
                stage(step // TILES, (step % TILES) // 2)

        def for_batch(stage, step):
            if 0 <= step < STEPS and step % TILES == 0:
                stage(step // TILES)

        def but_last(stage, step):
            if step < LAST * TILES:
                for_tile(stage, step)

        def for_last_pair(stage, step):
            if LAST * TILES <= step < STEPS and step % 2 == 0:
                for u in range(2):
                    stage(LAST, step % TILES + u)

        for i in range(-12, STEPS + 8):
            for_batch(load_features, i + 12)
            if i == -12:
                nc.sync.dma_start(out=w_rows[:], in_=wv2.rearrange("(ct p) ci -> p ct ci", p=P))
                nc.sync.dma_start(out=bias_row[0:1, :], in_=bv2.unsqueeze(0))
            for_batch(load_queries_keys, i + 9)
            if i == -9:
                nc.sync.dma_start(out=gamma_bf[:], in_=gamma.partition_broadcast(P))
            for_batch(load_residual, i)
            for_tile(scores, i + 1)
            but_last(scale, i - 7)
            but_last(add_residual, i - 7)
            for_batch(regroup_features, i + 8)
            for_pair(quantise_e, i - 3)
            for_batch(quantise_values, i - 2)
            for_batch(quantise_features, i + 5)
            if i == -5:
                prepare_weights()
            for_pair(invert_row_sums, i - 2)
            for_tile(row_maximum, i + 1)
            for_tile(value_rows, i + 3)
            but_last(attend, i - 6)
            for_pair(turn_e, i - 2)
            for_pair(turn_values, i + 1)
            for_tile(exponentials, i)
            for_batch(transpose_queries, i + 5)
            if i - 5 < LAST * TILES:
                for_batch(spread_factors, i - 5)
            for_last_pair(attend_rows, i - 4)
            for_last_pair(finish_rows, i - 6)
